import numpy as np
import ml_dtypes


def mxq(x, axis, fmt="e4m3"):
    dtype, down = {"e4m3": (ml_dtypes.float8_e4m3fn, 7), "e5m2": (ml_dtypes.float8_e5m2, 14)}[fmt]
    v = np.moveaxis(np.asarray(x, np.float32).astype(ml_dtypes.bfloat16).astype(np.float64), axis, -1)
    blocks = v.reshape(v.shape[:-1] + (-1, 32))
    amax = np.abs(blocks).max(-1, keepdims=True)
    byte = np.maximum(np.where(amax > 0, np.frexp(amax)[1] - 1 + 127, 0) - down, 1)
    scale = np.exp2(byte - 127.0)
    codes = (blocks / scale).astype(np.float32).astype(dtype).astype(np.float64)
    return np.moveaxis((codes * scale).reshape(v.shape), -1, axis)


WIDE = False


def mx_kscale(k):
    if not WIDE:
        return np.ones(k)
    levels = np.array([10, -10, 5, -5, 0])
    a = np.random.permutation(np.resize(levels, k // 512 * 4)).reshape(k // 512, 4)
    idx = np.arange(k)
    return np.exp2(a[idx // 512, idx % 128 // 32])


BF16 = ml_dtypes.bfloat16


def bf(x):
    return np.asarray(x, np.float32).astype(BF16)


def f64(x):
    return np.asarray(x).astype(np.float64)


B, T, DM, DH, L = 4, 1024, 512, 512, 512


def sigmoid(x):
    return 1.0 / (1.0 + np.exp(-x))


def setup_inputs():
    s, t = mx_kscale(DM), mx_kscale(DH)
    return {"q": bf(np.random.standard_normal((B, T, DM)) * s),
            "num": bf(np.random.standard_normal((B, T, DH)) * 1.9 * np.sqrt(T) * t),
            "den": bf(0.5 * T * (0.5 + np.random.random((B, T, DH)))),
            "Wq": bf(np.random.standard_normal((DH, DM)) / np.sqrt(DM) / s),
            "Wo": bf(np.random.standard_normal((DM, DH)) * 5.0 / np.sqrt(DH) / t)}


def reference(q, num, den, Wq, Wo):
    Q = mxq(f64(q), 2, "e4m3") @ mxq(f64(Wq), 1, "e4m3").T
    Yt = sigmoid(Q) * f64(num) / f64(den)
    return mxq(Yt, 2, "e4m3") @ mxq(f64(Wo), 1, "e4m3").T

@@ -1,0 +1,258 @@
+from contextlib import ExitStack
+
+import concourse.mybir as mybir
+from concourse.masks import make_identity
+
+BF16 = mybir.dt.bfloat16
+F32 = mybir.dt.float32
+U32 = mybir.dt.uint32
+U8 = mybir.dt.uint8
+FP8X4 = mybir.dt.float8_e4m3fn_x4
+FUNC = mybir.ActivationFunctionType
+MULT = mybir.AluOpType.mult
+
+P = 128
+PACK = 4
+WIDTH = P * PACK
+TOKENS = 4 * 1024
+SUB = 4
+CHUNK = P * SUB
+CHUNKS = TOKENS // CHUNK
+ROW = SUB * WIDTH
+BANK = 512
+LEAD = 3
+Q_BUFS = LEAD + 1
+
+FLOPS = 2 * 2 * TOKENS * WIDTH * WIDTH
+
+
+def tile_aftfull_pb_t_kernel(tc, q, num, den, Wq, Wo, out):
+    nc = tc.nc
+    by_chunk = "(c p j) w -> c p (j w)"
+    q_chunks = q.flatten_outer_dims().rearrange(by_chunk, p=P, j=SUB)
+    num_chunks = num.flatten_outer_dims().rearrange(by_chunk, p=P, j=SUB)
+    den_chunks = den.flatten_outer_dims().rearrange(by_chunk, p=P, j=SUB)
+    out_groups = out.flatten_outer_dims().rearrange("(c p j) w -> c j p w", p=P, j=SUB)
+
+    with ExitStack() as ctx:
+        keep = ctx.enter_context(tc.tile_pool(name="keep", bufs=1))
+        loads = ctx.enter_context(tc.tile_pool(name="loads", bufs=CHUNKS))
+        work = ctx.enter_context(tc.tile_pool(name="work", bufs=2))
+        psum = ctx.enter_context(tc.psum_pool(name="psum", bufs=8))
+        ctx.enter_context(tc.manual_schedule())
+
+        def load(source, tag, bufs):
+            rows = loads.tile([P, ROW], BF16, tag=tag, bufs=bufs)
+            nc.sync.dma_start(out=rows[:], in_=source)
+            return rows
+
+        def load_weight(weight, tag):
+            rows = loads.tile([P, ROW], BF16, tag=tag, bufs=1)
+            nc.sync.dma_start(
+                out=rows[:].rearrange("p (a k) -> p a k", a=SUB),
+                in_=weight.rearrange("(a p) k -> p a k", p=P),
+            )
+            return rows
+
+        den_rows = [load(den_chunks[c], "den", CHUNKS) for c in range(CHUNKS)]
+        wq_rows = load_weight(Wq, "wq")
+        wo_rows = load_weight(Wo, "wo")
+        q_rows = [load(q_chunks[c], "q", Q_BUFS) for c in range(LEAD)]
+        num_rows = [load(num_chunks[c], "num", CHUNKS) for c in range(LEAD)]
+        for c in range(LEAD, CHUNKS):
+            q_rows.append(load(q_chunks[c], "q", Q_BUFS))
+            num_rows.append(load(num_chunks[c], "num", CHUNKS))
+
+        ident_f32 = keep.tile([P, P], F32)
+        make_identity(nc, ident_f32[:])
+        ident_bf16 = keep.tile([P, P], BF16)
+        make_identity(nc, ident_bf16[:])
+
+        wq_codes = keep.tile([P, WIDTH], U32, align_bytes=64)
+        wq_scales = keep.tile([P, WIDTH], U8, align_bytes=64)
+        wo_codes = keep.tile([P, WIDTH], U32, align_bytes=64)
+        wo_scales = keep.tile([P, WIDTH], U8, align_bytes=64)
+        q_codes = keep.tile([P, TOKENS], U32, align_bytes=64)
+        q_scales = keep.tile([P, TOKENS], U8, align_bytes=64)
+
+        def quantise(grouped, codes, scales):
+            nc.vector.quantize_mx(out=codes.bitcast(FP8X4), scales=scales, in_=grouped)
+
+        def copy_on(on_scalar, out, in_):
+            if on_scalar:
+                nc.scalar.copy(out=out, in_=in_)
+            else:
+                nc.vector.tensor_copy(out=out, in_=in_)
+
+        def turn_features_last(rows, on_scalar):
+            words = rows[:].bitcast(F32)
+            grouped = work.tile([P, WIDTH * PACK], BF16, tag="grouped", bufs=LEAD, align_bytes=64)
+            grouped_words = grouped[:].bitcast(F32)
+            for half in range(2):
+                turned = psum.tile([P, BANK], F32, tag="bank")
+                for j in range(2):
+                    for u in range(2):
+                        first = (2 * half + j) * (WIDTH // 2) + u * P
+                        nc.tensor.transpose(
+                            turned[:, (2 * j + u) * P : (2 * j + u + 1) * P],
+                            words[:, first : first + P],
+                            ident_f32[:],
+                        )
+                copy_on(
+                    on_scalar,
+                    grouped_words[:, half * BANK : (half + 1) * BANK].rearrange(
+                        "p (j r u) -> p j r u", j=2, u=2
+                    ),
+                    turned[:].rearrange("p (j u r) -> p j r u", j=2, u=2),
+                )
+            return grouped
+
+        def turn_wo():
+            grouped = work.tile([P, WIDTH * PACK], BF16, tag="grouped", bufs=LEAD, align_bytes=64)
+            for half in range(2):
+                turned = psum.tile([P, 2 * BANK], BF16, tag="bank")
+                for j in range(2):
+                    for t in range(PACK):
+                        first = (2 * half + j) * WIDTH + t * P
+                        nc.tensor.transpose(
+                            turned[:, (2 * t + j) * P : (2 * t + j + 1) * P],
+                            wo_rows[:, first : first + P],
+                            ident_bf16[:],
+                        )
+                nc.vector.tensor_copy(
+                    out=grouped[:, half * 2 * BANK : (half + 1) * 2 * BANK].rearrange(
+                        "p (o t) -> p o t", t=PACK
+                    ),
+                    in_=turned[:].rearrange("p (t o) -> p o t", t=PACK),
+                )
+            return grouped
+
+        def chunk_columns(c):
+            return slice(c * CHUNK, (c + 1) * CHUNK)
+
+        ratio_tiles = []
+
+        def root_of_den(c):
+            ratio = loads.tile([P, ROW], F32, tag="ratio")
+            nc.scalar.activation(out=ratio[:], in_=den_rows[c][:], func=FUNC.Abs_reciprocal_sqrt)
+            ratio_tiles.append(ratio)
+
+        def square_root_of_den(c, on_scalar):
+            ratio = ratio_tiles[c]
+            if on_scalar:
+                nc.scalar.activation(out=ratio[:], in_=ratio[:], func=FUNC.Square)
+            else:
+                nc.vector.tensor_tensor(out=ratio[:], in0=ratio[:], in1=ratio[:], op=MULT)
+
+        def finish_ratio(c):
+            ratio = ratio_tiles[c]
+            nc.vector.tensor_tensor(out=ratio[:], in0=num_rows[c][:], in1=ratio[:], op=MULT)
+
+        grouped_q = {}
+
+        def turn_q(c, on_scalar):
+            grouped_q[c] = turn_features_last(q_rows[c], on_scalar)
+
+        def quantise_q(c):
+            quantise(grouped_q[c][:], q_codes[:, chunk_columns(c)], q_scales[:, chunk_columns(c)])
+
+        gate_tiles = {}
+
+        def project(c):
+            gate = work.tile([P, PACK, CHUNK], F32, tag="gate")
+            for a in range(PACK):
+                acc = psum.tile([P, BANK], F32, tag="bank")
+                nc.tensor.matmul_mx(
+                    out=acc[:],
+                    lhsT=wq_codes[:, a * P : (a + 1) * P].bitcast(FP8X4),
+                    lhsT_scale=wq_scales[:, a * P : (a + 1) * P],
+                    rhs=q_codes[:, chunk_columns(c)].bitcast(FP8X4),
+                    rhs_scale=q_scales[:, chunk_columns(c)],
+                    start=True,
+                    stop=True,
+                )
+                nc.scalar.activation(out=gate[:, a, :], in_=acc[:], func=FUNC.Sigmoid)
+            gate_tiles[c] = gate
+
+        turned_ratios = {}
+
+        def turn_ratio(c):
+            for j in range(SUB):
+                turned = psum.tile([P, PACK, P], F32, tag="bank")
+                for a in range(PACK):
+                    first = j * WIDTH + a * P
+                    nc.tensor.transpose(turned[:, a, :], ratio_tiles[c][:, first : first + P], ident_f32[:])
+                turned_ratios[(c, j)] = turned
+
+        grouped_y = {}
+
+        def apply_gate(c):
+            grouped = work.tile([P, CHUNK, PACK], BF16, tag="y", align_bytes=64)
+            for j in range(SUB):
+                tokens = slice(j * P, (j + 1) * P)
+                nc.vector.tensor_tensor(
+                    out=grouped[:, tokens, :],
+                    in0=gate_tiles[c][:, :, tokens].rearrange("p a r -> p r a"),
+                    in1=turned_ratios[(c, j)][:].rearrange("p a r -> p r a"),
+                    op=MULT,
+                )
+            grouped_y[c] = grouped
+
+        y_tiles = {}
+
+        def quantise_y(c):
+            y_codes = work.tile([P, CHUNK], U32, tag="y_codes", align_bytes=64)
+            y_scales = work.tile([P, CHUNK], U8, tag="y_scales", align_bytes=64)
+            quantise(grouped_y[c][:].rearrange("p r a -> p (r a)"), y_codes[:], y_scales[:])
+            y_tiles[c] = (y_codes, y_scales)
+
+        def project_out(c):
+            y_codes, y_scales = y_tiles[c]
+            for j in range(SUB):
+                acc = psum.tile([P, BANK], F32, tag="bank")
+                nc.tensor.matmul_mx(
+                    out=acc[:],
+                    lhsT=y_codes[:, j * P : (j + 1) * P].bitcast(FP8X4),
+                    lhsT_scale=y_scales[:, j * P : (j + 1) * P],
+                    rhs=wo_codes[:].bitcast(FP8X4),
+                    rhs_scale=wo_scales[:],
+                    start=True,
+                    stop=True,
+                )
+                result = work.tile([P, WIDTH], F32, tag="result", bufs=6)
+                copy_on(j % 2 == 0, result[:], acc[:])
+                nc.sync.dma_start(out=out_groups[c, j], in_=result[:])
+
+        for c in range(CHUNKS):
+            root_of_den(c)
+        for c in range(LEAD):
+            square_root_of_den(c, on_scalar=False)
+        grouped_wq = turn_features_last(wq_rows, on_scalar=False)
+        grouped_wo = turn_wo()
+        quantise(grouped_wq[:], wq_codes[:], wq_scales[:])
+        quantise(grouped_wo[:], wo_codes[:], wo_scales[:])
+        for c in range(LEAD):
+            turn_q(c, on_scalar=False)
+        for c in range(LEAD):
+            quantise_q(c)
+        for c in range(LEAD):
+            finish_ratio(c)
+        project(0)
+        project(1)
+        turn_ratio(0)
+        for c in range(CHUNKS):
+            ahead = c + LEAD
+            apply_gate(c)
+            if ahead < CHUNKS:
+                turn_q(ahead, on_scalar=True)
+            if c + 1 < CHUNKS:
+                turn_ratio(c + 1)
+            quantise_y(c)
+            if ahead < CHUNKS:
+                square_root_of_den(ahead, on_scalar=True)
+            project_out(c)
+            if c + 2 < CHUNKS:
+                project(c + 2)
+            if ahead < CHUNKS:
+                finish_ratio(ahead)
+                quantise_q(ahead)

@@ -15,13 +15,12 @@ P = 128
 PACK = 4
 WIDTH = P * PACK
 TOKENS = 4 * 1024
+GROUPS = TOKENS // P
 SUB = 4
-CHUNK = P * SUB
-CHUNKS = TOKENS // CHUNK
+CHUNKS = GROUPS // SUB
 ROW = SUB * WIDTH
 BANK = 512
-LEAD = 3
-Q_BUFS = LEAD + 1
+LEAD = 8
 
 FLOPS = 2 * 2 * TOKENS * WIDTH * WIDTH
 
@@ -37,12 +36,12 @@ def tile_aftfull_pb_t_kernel(tc, q, num, den, Wq, Wo, out):
     with ExitStack() as ctx:
         keep = ctx.enter_context(tc.tile_pool(name="keep", bufs=1))
         loads = ctx.enter_context(tc.tile_pool(name="loads", bufs=CHUNKS))
-        work = ctx.enter_context(tc.tile_pool(name="work", bufs=2))
-        psum = ctx.enter_context(tc.psum_pool(name="psum", bufs=8))
+        work = ctx.enter_context(tc.tile_pool(name="work", bufs=4))
+        psum = ctx.enter_context(tc.psum_pool(name="psum", bufs=2))
         ctx.enter_context(tc.manual_schedule())
 
-        def load(source, tag, bufs):
-            rows = loads.tile([P, ROW], BF16, tag=tag, bufs=bufs)
+        def load(source, tag):
+            rows = loads.tile([P, ROW], BF16, tag=tag)
             nc.sync.dma_start(out=rows[:], in_=source)
             return rows
 
@@ -54,14 +53,15 @@ def tile_aftfull_pb_t_kernel(tc, q, num, den, Wq, Wo, out):
             )
             return rows
 
-        den_rows = [load(den_chunks[c], "den", CHUNKS) for c in range(CHUNKS)]
+        first_chunks = LEAD // SUB
+        den_rows = [load(den_chunks[c], "den") for c in range(CHUNKS)]
         wq_rows = load_weight(Wq, "wq")
         wo_rows = load_weight(Wo, "wo")
-        q_rows = [load(q_chunks[c], "q", Q_BUFS) for c in range(LEAD)]
-        num_rows = [load(num_chunks[c], "num", CHUNKS) for c in range(LEAD)]
-        for c in range(LEAD, CHUNKS):
-            q_rows.append(load(q_chunks[c], "q", Q_BUFS))
-            num_rows.append(load(num_chunks[c], "num", CHUNKS))
+        q_rows = [load(q_chunks[c], "q") for c in range(first_chunks)]
+        num_rows = [load(num_chunks[c], "num") for c in range(first_chunks)]
+        for c in range(first_chunks, CHUNKS):
+            q_rows.append(load(q_chunks[c], "q"))
+            num_rows.append(load(num_chunks[c], "num"))
 
         ident_f32 = keep.tile([P, P], F32)
         make_identity(nc, ident_f32[:])
@@ -84,51 +84,45 @@ def tile_aftfull_pb_t_kernel(tc, q, num, den, Wq, Wo, out):
             else:
                 nc.vector.tensor_copy(out=out, in_=in_)
 
-        def turn_features_last(rows, on_scalar):
-            words = rows[:].bitcast(F32)
-            grouped = work.tile([P, WIDTH * PACK], BF16, tag="grouped", bufs=LEAD, align_bytes=64)
-            grouped_words = grouped[:].bitcast(F32)
-            for half in range(2):
-                turned = psum.tile([P, BANK], F32, tag="bank")
-                for j in range(2):
-                    for u in range(2):
-                        first = (2 * half + j) * (WIDTH // 2) + u * P
-                        nc.tensor.transpose(
-                            turned[:, (2 * j + u) * P : (2 * j + u + 1) * P],
-                            words[:, first : first + P],
-                            ident_f32[:],
-                        )
-                copy_on(
-                    on_scalar,
-                    grouped_words[:, half * BANK : (half + 1) * BANK].rearrange(
-                        "p (j r u) -> p j r u", j=2, u=2
-                    ),
-                    turned[:].rearrange("p (j u r) -> p j r u", j=2, u=2),
-                )
+        def columns(g):
+            return slice(g * P, (g + 1) * P)
+
+        def in_chunk(tiles, g):
+            return tiles[g // SUB][:, (g % SUB) * WIDTH : (g % SUB + 1) * WIDTH]
+
+        def turn_pairs(rows):
+            words = rows.bitcast(F32)
+            turned = psum.tile([P, 2, P], F32, tag="turned_pairs")
+            for u in range(2):
+                nc.tensor.transpose(turned[:, u, :], words[:, u * P : (u + 1) * P], ident_f32[:])
+            return turned
+
+        def group_pairs(turned, grouped, on_scalar):
+            copy_on(
+                on_scalar,
+                grouped.bitcast(F32).rearrange("p (r u) -> p r u", u=2),
+                turned[:].rearrange("p u r -> p r u"),
+            )
+
+        def group_wq():
+            grouped = work.tile([P, WIDTH * PACK], BF16, tag="grouped_w", bufs=2, align_bytes=64)
+            for a in range(SUB):
+                turned = turn_pairs(wq_rows[:, a * WIDTH : (a + 1) * WIDTH])
+                group_pairs(turned, grouped[:, a * WIDTH : (a + 1) * WIDTH], on_scalar=False)
             return grouped
 
-        def turn_wo():
-            grouped = work.tile([P, WIDTH * PACK], BF16, tag="grouped", bufs=LEAD, align_bytes=64)
-            for half in range(2):
-                turned = psum.tile([P, 2 * BANK], BF16, tag="bank")
-                for j in range(2):
-                    for t in range(PACK):
-                        first = (2 * half + j) * WIDTH + t * P
-                        nc.tensor.transpose(
-                            turned[:, (2 * t + j) * P : (2 * t + j + 1) * P],
-                            wo_rows[:, first : first + P],
-                            ident_bf16[:],
-                        )
+        def group_wo():
+            grouped = work.tile([P, WIDTH * PACK], BF16, tag="grouped_w", bufs=2, align_bytes=64)
+            for a in range(SUB):
+                turned = psum.tile([P, PACK, P], BF16, tag="turned_pairs")
+                for t in range(PACK):
+                    first = a * WIDTH + t * P
+                    nc.tensor.transpose(turned[:, t, :], wo_rows[:, first : first + P], ident_bf16[:])
                 nc.vector.tensor_copy(
-                    out=grouped[:, half * 2 * BANK : (half + 1) * 2 * BANK].rearrange(
-                        "p (o t) -> p o t", t=PACK
-                    ),
-                    in_=turned[:].rearrange("p (t o) -> p o t", t=PACK),
+                    out=grouped[:, a * WIDTH : (a + 1) * WIDTH].rearrange("p (o t) -> p o t", t=PACK),
+                    in_=turned[:].rearrange("p t o -> p o t"),
                 )
             return grouped
-
-        def chunk_columns(c):
-            return slice(c * CHUNK, (c + 1) * CHUNK)
 
         ratio_tiles = []
 
@@ -137,122 +131,138 @@ def tile_aftfull_pb_t_kernel(tc, q, num, den, Wq, Wo, out):
             nc.scalar.activation(out=ratio[:], in_=den_rows[c][:], func=FUNC.Abs_reciprocal_sqrt)
             ratio_tiles.append(ratio)
 
-        def square_root_of_den(c, on_scalar):
-            ratio = ratio_tiles[c]
+        def square_root_of_den(g, on_scalar):
+            ratio = in_chunk(ratio_tiles, g)
             if on_scalar:
-                nc.scalar.activation(out=ratio[:], in_=ratio[:], func=FUNC.Square)
+                nc.scalar.activation(out=ratio, in_=ratio, func=FUNC.Square)
             else:
-                nc.vector.tensor_tensor(out=ratio[:], in0=ratio[:], in1=ratio[:], op=MULT)
+                nc.vector.tensor_tensor(out=ratio, in0=ratio, in1=ratio, op=MULT)
 
-        def finish_ratio(c):
-            ratio = ratio_tiles[c]
-            nc.vector.tensor_tensor(out=ratio[:], in0=num_rows[c][:], in1=ratio[:], op=MULT)
+        def finish_ratio(g):
+            ratio = in_chunk(ratio_tiles, g)
+            nc.vector.tensor_tensor(out=ratio, in0=in_chunk(num_rows, g), in1=ratio, op=MULT)
 
-        grouped_q = {}
+        turned_q, grouped_q = {}, {}
 
-        def turn_q(c, on_scalar):
-            grouped_q[c] = turn_features_last(q_rows[c], on_scalar)
+        def turn_q(g):
+            turned_q[g] = turn_pairs(in_chunk(q_rows, g))
 
-        def quantise_q(c):
-            quantise(grouped_q[c][:], q_codes[:, chunk_columns(c)], q_scales[:, chunk_columns(c)])
+        def group_q(g, on_scalar):
+            grouped = work.tile([P, WIDTH], BF16, tag="grouped_q", align_bytes=64)
+            group_pairs(turned_q[g], grouped[:], on_scalar)
+            grouped_q[g] = grouped
 
-        gate_tiles = {}
+        def quantise_q(g):
+            quantise(grouped_q[g][:], q_codes[:, columns(g)], q_scales[:, columns(g)])
 
-        def project(c):
-            gate = work.tile([P, PACK, CHUNK], F32, tag="gate")
+        products, gates, turned_ratios, grouped_y, y_operands, results = {}, {}, {}, {}, {}, {}
+
+        def first_product(g):
+            acc = psum.tile([P, PACK, P], F32, tag="first_product")
             for a in range(PACK):
-                acc = psum.tile([P, BANK], F32, tag="bank")
                 nc.tensor.matmul_mx(
-                    out=acc[:],
-                    lhsT=wq_codes[:, a * P : (a + 1) * P].bitcast(FP8X4),
-                    lhsT_scale=wq_scales[:, a * P : (a + 1) * P],
-                    rhs=q_codes[:, chunk_columns(c)].bitcast(FP8X4),
-                    rhs_scale=q_scales[:, chunk_columns(c)],
+                    out=acc[:, a, :],
+                    lhsT=wq_codes[:, columns(a)].bitcast(FP8X4),
+                    lhsT_scale=wq_scales[:, columns(a)],
+                    rhs=q_codes[:, columns(g)].bitcast(FP8X4),
+                    rhs_scale=q_scales[:, columns(g)],
                     start=True,
                     stop=True,
                 )
-                nc.scalar.activation(out=gate[:, a, :], in_=acc[:], func=FUNC.Sigmoid)
-            gate_tiles[c] = gate
+            products[g] = acc
 
-        turned_ratios = {}
+        def sigmoid(g):
+            gate = work.tile([P, PACK, P], F32, tag="gate")
+            nc.scalar.activation(out=gate[:], in_=products[g][:], func=FUNC.Sigmoid)
+            gates[g] = gate
 
-        def turn_ratio(c):
-            for j in range(SUB):
-                turned = psum.tile([P, PACK, P], F32, tag="bank")
-                for a in range(PACK):
-                    first = j * WIDTH + a * P
-                    nc.tensor.transpose(turned[:, a, :], ratio_tiles[c][:, first : first + P], ident_f32[:])
-                turned_ratios[(c, j)] = turned
+        def turn_ratio(g):
+            ratio = in_chunk(ratio_tiles, g)
+            turned = psum.tile([P, PACK, P], F32, tag="turned_ratio")
+            for a in range(PACK):
+                nc.tensor.transpose(turned[:, a, :], ratio[:, columns(a)], ident_f32[:])
+            turned_ratios[g] = turned
 
-        grouped_y = {}
+        def apply_gate(g):
+            grouped = work.tile([P, P, PACK], BF16, tag="grouped_y", align_bytes=64)
+            nc.vector.tensor_tensor(
+                out=grouped[:],
+                in0=gates[g][:].rearrange("p a r -> p r a"),
+                in1=turned_ratios[g][:].rearrange("p a r -> p r a"),
+                op=MULT,
+            )
+            grouped_y[g] = grouped
 
-        def apply_gate(c):
-            grouped = work.tile([P, CHUNK, PACK], BF16, tag="y", align_bytes=64)
-            for j in range(SUB):
-                tokens = slice(j * P, (j + 1) * P)
-                nc.vector.tensor_tensor(
-                    out=grouped[:, tokens, :],
-                    in0=gate_tiles[c][:, :, tokens].rearrange("p a r -> p r a"),
-                    in1=turned_ratios[(c, j)][:].rearrange("p a r -> p r a"),
-                    op=MULT,
-                )
-            grouped_y[c] = grouped
+        def quantise_y(g):
+            y_codes = work.tile([P, P], U32, tag="y_codes", align_bytes=64)
+            y_scales = work.tile([P, P], U8, tag="y_scales", align_bytes=64)
+            quantise(grouped_y[g][:].rearrange("p r a -> p (r a)"), y_codes[:], y_scales[:])
+            y_operands[g] = (y_codes, y_scales)
 
-        y_tiles = {}
+        def second_product(g):
+            y_codes, y_scales = y_operands[g]
+            acc = psum.tile([P, BANK], F32, tag="second_product")
+            nc.tensor.matmul_mx(
+                out=acc[:],
+                lhsT=y_codes[:].bitcast(FP8X4),
+                lhsT_scale=y_scales[:],
+                rhs=wo_codes[:].bitcast(FP8X4),
+                rhs_scale=wo_scales[:],
+                start=True,
+                stop=True,
+            )
+            results[g] = acc
 
-        def quantise_y(c):
-            y_codes = work.tile([P, CHUNK], U32, tag="y_codes", align_bytes=64)
-            y_scales = work.tile([P, CHUNK], U8, tag="y_scales", align_bytes=64)
-            quantise(grouped_y[c][:].rearrange("p r a -> p (r a)"), y_codes[:], y_scales[:])
-            y_tiles[c] = (y_codes, y_scales)
-
-        def project_out(c):
-            y_codes, y_scales = y_tiles[c]
-            for j in range(SUB):
-                acc = psum.tile([P, BANK], F32, tag="bank")
-                nc.tensor.matmul_mx(
-                    out=acc[:],
-                    lhsT=y_codes[:, j * P : (j + 1) * P].bitcast(FP8X4),
-                    lhsT_scale=y_scales[:, j * P : (j + 1) * P],
-                    rhs=wo_codes[:].bitcast(FP8X4),
-                    rhs_scale=wo_scales[:],
-                    start=True,
-                    stop=True,
-                )
-                result = work.tile([P, WIDTH], F32, tag="result", bufs=6)
-                copy_on(j % 2 == 0, result[:], acc[:])
-                nc.sync.dma_start(out=out_groups[c, j], in_=result[:])
+        def store(g):
+            result = work.tile([P, WIDTH], F32, tag="result")
+            copy_on(g % 2 == 0, result[:], results[g][:])
+            nc.sync.dma_start(out=out_groups[g // SUB, g % SUB], in_=result[:])
 
         for c in range(CHUNKS):
             root_of_den(c)
-        for c in range(LEAD):
-            square_root_of_den(c, on_scalar=False)
-        grouped_wq = turn_features_last(wq_rows, on_scalar=False)
-        grouped_wo = turn_wo()
+        for g in range(LEAD):
+            square_root_of_den(g, on_scalar=False)
+        grouped_wq = group_wq()
+        grouped_wo = group_wo()
         quantise(grouped_wq[:], wq_codes[:], wq_scales[:])
         quantise(grouped_wo[:], wo_codes[:], wo_scales[:])
-        for c in range(LEAD):
-            turn_q(c, on_scalar=False)
-        for c in range(LEAD):
-            quantise_q(c)
-        for c in range(LEAD):
-            finish_ratio(c)
-        project(0)
-        project(1)
-        turn_ratio(0)
-        for c in range(CHUNKS):
-            ahead = c + LEAD
-            apply_gate(c)
-            if ahead < CHUNKS:
-                turn_q(ahead, on_scalar=True)
-            if c + 1 < CHUNKS:
-                turn_ratio(c + 1)
-            quantise_y(c)
-            if ahead < CHUNKS:
-                square_root_of_den(ahead, on_scalar=True)
-            project_out(c)
-            if c + 2 < CHUNKS:
-                project(c + 2)
-            if ahead < CHUNKS:
-                finish_ratio(ahead)
-                quantise_q(ahead)
+        for g in range(LEAD):
+            turn_q(g)
+            group_q(g, on_scalar=False)
+            if g > 0:
+                quantise_q(g - 1)
+        quantise_q(LEAD - 1)
+        for g in range(LEAD):
+            finish_ratio(g)
+
+        def is_group(g):
+            return 0 <= g < GROUPS
+
+        def is_new(g):
+            return LEAD <= g < GROUPS
+
+        for r in range(-2, GROUPS + 2):
+            new = r + LEAD
+            if is_new(new + 1):
+                turn_q(new + 1)
+            if is_group(r + 1):
+                turn_ratio(r + 1)
+            if is_group(r - 1):
+                second_product(r - 1)
+            if is_group(r + 2):
+                first_product(r + 2)
+            if is_group(r + 1):
+                sigmoid(r + 1)
+            if is_group(r):
+                apply_gate(r)
+            if is_new(new):
+                square_root_of_den(new, on_scalar=True)
+                group_q(new, on_scalar=True)
+            if is_new(new - 1):
+                finish_ratio(new - 1)
+            if is_group(r):
+                quantise_y(r)
+            if is_new(new - 1):
+                quantise_q(new - 1)
+            if is_group(r - 2):
+                store(r - 2)

@@ -20,7 +20,7 @@ SUB = 4
 CHUNKS = GROUPS // SUB
 ROW = SUB * WIDTH
 BANK = 512
-LEAD = 8
+LEAD = 12
 
 FLOPS = 2 * 2 * TOKENS * WIDTH * WIDTH
 
@@ -53,15 +53,15 @@ def tile_aftfull_pb_t_kernel(tc, q, num, den, Wq, Wo, out):
             )
             return rows
 
-        first_chunks = LEAD // SUB
-        den_rows = [load(den_chunks[c], "den") for c in range(CHUNKS)]
+        den_rows = [load(den_chunks[c], "den") for c in range(2)]
         wq_rows = load_weight(Wq, "wq")
         wo_rows = load_weight(Wo, "wo")
-        q_rows = [load(q_chunks[c], "q") for c in range(first_chunks)]
-        num_rows = [load(num_chunks[c], "num") for c in range(first_chunks)]
-        for c in range(first_chunks, CHUNKS):
-            q_rows.append(load(q_chunks[c], "q"))
+        for c in range(2, CHUNKS):
+            den_rows.append(load(den_chunks[c], "den"))
+        num_rows, q_rows = [], []
+        for c in range(CHUNKS):
             num_rows.append(load(num_chunks[c], "num"))
+            q_rows.append(load(q_chunks[c], "q"))
 
         ident_f32 = keep.tile([P, P], F32)
         make_identity(nc, ident_f32[:])
@@ -97,18 +97,17 @@ def tile_aftfull_pb_t_kernel(tc, q, num, den, Wq, Wo, out):
                 nc.tensor.transpose(turned[:, u, :], words[:, u * P : (u + 1) * P], ident_f32[:])
             return turned
 
-        def group_pairs(turned, grouped, on_scalar):
-            copy_on(
-                on_scalar,
-                grouped.bitcast(F32).rearrange("p (r u) -> p r u", u=2),
-                turned[:].rearrange("p u r -> p r u"),
+        def group_pairs(turned, grouped):
+            nc.vector.tensor_copy(
+                out=grouped.bitcast(F32).rearrange("p (r u) -> p r u", u=2),
+                in_=turned[:].rearrange("p u r -> p r u"),
             )
 
         def group_wq():
             grouped = work.tile([P, WIDTH * PACK], BF16, tag="grouped_w", bufs=2, align_bytes=64)
             for a in range(SUB):
                 turned = turn_pairs(wq_rows[:, a * WIDTH : (a + 1) * WIDTH])
-                group_pairs(turned, grouped[:, a * WIDTH : (a + 1) * WIDTH], on_scalar=False)
+                group_pairs(turned, grouped[:, a * WIDTH : (a + 1) * WIDTH])
             return grouped
 
         def group_wo():
@@ -140,16 +139,16 @@ def tile_aftfull_pb_t_kernel(tc, q, num, den, Wq, Wo, out):
 
         def finish_ratio(g):
             ratio = in_chunk(ratio_tiles, g)
-            nc.vector.tensor_tensor(out=ratio, in0=in_chunk(num_rows, g), in1=ratio, op=MULT)
+            nc.gpsimd.tensor_tensor(out=ratio, in0=in_chunk(num_rows, g), in1=ratio, op=MULT)
 
         turned_q, grouped_q = {}, {}
 
         def turn_q(g):
             turned_q[g] = turn_pairs(in_chunk(q_rows, g))
 
-        def group_q(g, on_scalar):
+        def group_q(g):
             grouped = work.tile([P, WIDTH], BF16, tag="grouped_q", align_bytes=64)
-            group_pairs(turned_q[g], grouped[:], on_scalar)
+            group_pairs(turned_q[g], grouped[:])
             grouped_q[g] = grouped
 
         def quantise_q(g):
@@ -172,8 +171,10 @@ def tile_aftfull_pb_t_kernel(tc, q, num, den, Wq, Wo, out):
             products[g] = acc
 
         def sigmoid(g):
-            gate = work.tile([P, PACK, P], F32, tag="gate")
-            nc.scalar.activation(out=gate[:], in_=products[g][:], func=FUNC.Sigmoid)
+            gate = work.tile([P, P, PACK], F32, tag="gate")
+            nc.scalar.activation(
+                out=gate[:], in_=products[g][:].rearrange("p a r -> p r a"), func=FUNC.Sigmoid
+            )
             gates[g] = gate
 
         def turn_ratio(g):
@@ -187,7 +188,7 @@ def tile_aftfull_pb_t_kernel(tc, q, num, den, Wq, Wo, out):
             grouped = work.tile([P, P, PACK], BF16, tag="grouped_y", align_bytes=64)
             nc.vector.tensor_tensor(
                 out=grouped[:],
-                in0=gates[g][:].rearrange("p a r -> p r a"),
+                in0=gates[g][:],
                 in1=turned_ratios[g][:].rearrange("p a r -> p r a"),
                 op=MULT,
             )
@@ -220,20 +221,19 @@ def tile_aftfull_pb_t_kernel(tc, q, num, den, Wq, Wo, out):
 
         for c in range(CHUNKS):
             root_of_den(c)
-        for g in range(LEAD):
-            square_root_of_den(g, on_scalar=False)
         grouped_wq = group_wq()
         grouped_wo = group_wo()
         quantise(grouped_wq[:], wq_codes[:], wq_scales[:])
         quantise(grouped_wo[:], wo_codes[:], wo_scales[:])
         for g in range(LEAD):
+            square_root_of_den(g, on_scalar=False)
+            finish_ratio(g)
+        for g in range(LEAD):
             turn_q(g)
-            group_q(g, on_scalar=False)
+            group_q(g)
             if g > 0:
                 quantise_q(g - 1)
         quantise_q(LEAD - 1)
-        for g in range(LEAD):
-            finish_ratio(g)
 
         def is_group(g):
             return 0 <= g < GROUPS
@@ -257,7 +257,7 @@ def tile_aftfull_pb_t_kernel(tc, q, num, den, Wq, Wo, out):
                 apply_gate(r)
             if is_new(new):
                 square_root_of_den(new, on_scalar=True)
-                group_q(new, on_scalar=True)
+                group_q(new)
             if is_new(new - 1):
                 finish_ratio(new - 1)
             if is_group(r):

@@ -20,7 +20,8 @@ SUB = 4
 CHUNKS = GROUPS // SUB
 ROW = SUB * WIDTH
 BANK = 512
-LEAD = 12
+LEAD = 8
+QLEAD = 4
 
 FLOPS = 2 * 2 * TOKENS * WIDTH * WIDTH
 
@@ -40,8 +41,8 @@ def tile_aftfull_pb_t_kernel(tc, q, num, den, Wq, Wo, out):
         psum = ctx.enter_context(tc.psum_pool(name="psum", bufs=2))
         ctx.enter_context(tc.manual_schedule())
 
-        def load(source, tag):
-            rows = loads.tile([P, ROW], BF16, tag=tag)
+        def load(source, tag, bufs=CHUNKS):
+            rows = loads.tile([P, ROW], BF16, tag=tag, bufs=bufs)
             nc.sync.dma_start(out=rows[:], in_=source)
             return rows
 
@@ -53,15 +54,28 @@ def tile_aftfull_pb_t_kernel(tc, q, num, den, Wq, Wo, out):
             )
             return rows
 
-        den_rows = [load(den_chunks[c], "den") for c in range(2)]
-        wq_rows = load_weight(Wq, "wq")
-        wo_rows = load_weight(Wo, "wo")
-        for c in range(2, CHUNKS):
-            den_rows.append(load(den_chunks[c], "den"))
-        num_rows, q_rows = [], []
+        den_rows, num_rows, q_rows, weight_rows = [], [], [], {}
+
+        def fetch(what, c):
+            if what == "den":
+                den_rows.append(load(den_chunks[c], "den"))
+            elif what == "num":
+                if c < CHUNKS // 2:
+                    num_rows.append(load(num_chunks[c], "num", bufs=CHUNKS // 2))
+                else:
+                    num_rows.append(load(num_chunks[c], "den"))
+            elif what == "q":
+                q_rows.append(load(q_chunks[c], "q"))
+            elif what == "wq":
+                weight_rows["wq"] = load_weight(Wq, "wq")
+            else:
+                weight_rows["wo"] = load_weight(Wo, "wo")
+
+        between = [("wq", 0), ("q", 0), ("num", 0), ("q", 1), ("wo", 0), ("num", 1), ("q", 2), ("q", 3)]
         for c in range(CHUNKS):
-            num_rows.append(load(num_chunks[c], "num"))
-            q_rows.append(load(q_chunks[c], "q"))
+            fetch("den", c)
+            fetch(between[c][0], between[c][1])
+        wq_rows, wo_rows = weight_rows["wq"], weight_rows["wo"]
 
         ident_f32 = keep.tile([P, P], F32)
         make_identity(nc, ident_f32[:])
@@ -78,42 +92,41 @@ def tile_aftfull_pb_t_kernel(tc, q, num, den, Wq, Wo, out):
         def quantise(grouped, codes, scales):
             nc.vector.quantize_mx(out=codes.bitcast(FP8X4), scales=scales, in_=grouped)
 
-        def copy_on(on_scalar, out, in_):
-            if on_scalar:
-                nc.scalar.copy(out=out, in_=in_)
-            else:
-                nc.vector.tensor_copy(out=out, in_=in_)
-
         def columns(g):
             return slice(g * P, (g + 1) * P)
+
+        def chunk_columns(c):
+            return slice(c * WIDTH, (c + 1) * WIDTH)
 
         def in_chunk(tiles, g):
             return tiles[g // SUB][:, (g % SUB) * WIDTH : (g % SUB + 1) * WIDTH]
 
         def turn_pairs(rows):
             words = rows.bitcast(F32)
-            turned = psum.tile([P, 2, P], F32, tag="turned_pairs")
-            for u in range(2):
-                nc.tensor.transpose(turned[:, u, :], words[:, u * P : (u + 1) * P], ident_f32[:])
+            turned = psum.tile([P, 2, 2, P], F32, tag="turned", bufs=3)
+            for b in range(2):
+                for u in range(2):
+                    first = b * 2 * P + u * P
+                    nc.tensor.transpose(turned[:, b, u, :], words[:, first : first + P], ident_f32[:])
             return turned
 
         def group_pairs(turned, grouped):
             nc.vector.tensor_copy(
-                out=grouped.bitcast(F32).rearrange("p (r u) -> p r u", u=2),
-                in_=turned[:].rearrange("p u r -> p r u"),
+                out=grouped.bitcast(F32).rearrange("p (b r u) -> p b r u", b=2, u=2),
+                in_=turned[:].rearrange("p b u r -> p b r u"),
             )
 
         def group_wq():
-            grouped = work.tile([P, WIDTH * PACK], BF16, tag="grouped_w", bufs=2, align_bytes=64)
-            for a in range(SUB):
-                turned = turn_pairs(wq_rows[:, a * WIDTH : (a + 1) * WIDTH])
-                group_pairs(turned, grouped[:, a * WIDTH : (a + 1) * WIDTH])
+            grouped = work.tile([P, ROW], BF16, tag="grouped", bufs=3, align_bytes=64)
+            for h in range(2):
+                half = slice(h * 2 * WIDTH, (h + 1) * 2 * WIDTH)
+                group_pairs(turn_pairs(wq_rows[:, half]), grouped[:, half])
             return grouped
 
         def group_wo():
-            grouped = work.tile([P, WIDTH * PACK], BF16, tag="grouped_w", bufs=2, align_bytes=64)
+            grouped = work.tile([P, ROW], BF16, tag="grouped", bufs=3, align_bytes=64)
             for a in range(SUB):
-                turned = psum.tile([P, PACK, P], BF16, tag="turned_pairs")
+                turned = psum.tile([P, PACK, P], BF16, tag="turned", bufs=3)
                 for t in range(PACK):
                     first = a * WIDTH + t * P
                     nc.tensor.transpose(turned[:, t, :], wo_rows[:, first : first + P], ident_bf16[:])
@@ -139,25 +152,33 @@ def tile_aftfull_pb_t_kernel(tc, q, num, den, Wq, Wo, out):
 
         def finish_ratio(g):
             ratio = in_chunk(ratio_tiles, g)
-            nc.gpsimd.tensor_tensor(out=ratio, in0=in_chunk(num_rows, g), in1=ratio, op=MULT)
+            nums = in_chunk(num_rows, g)
+            nc.vector.tensor_tensor(out=ratio, in0=nums, in1=ratio, op=MULT)
+
+        def square_chunk(c):
+            nc.vector.tensor_tensor(out=ratio_tiles[c][:], in0=ratio_tiles[c][:], in1=ratio_tiles[c][:], op=MULT)
+
+        def finish_chunk(c):
+            nc.vector.tensor_tensor(out=ratio_tiles[c][:], in0=num_rows[c][:], in1=ratio_tiles[c][:], op=MULT)
 
         turned_q, grouped_q = {}, {}
 
-        def turn_q(g):
-            turned_q[g] = turn_pairs(in_chunk(q_rows, g))
+        def turn_q(c, h):
+            turned_q[c, h] = turn_pairs(q_rows[c][:, h * 2 * WIDTH : (h + 1) * 2 * WIDTH])
 
-        def group_q(g):
-            grouped = work.tile([P, WIDTH], BF16, tag="grouped_q", align_bytes=64)
-            group_pairs(turned_q[g], grouped[:])
-            grouped_q[g] = grouped
+        def group_q(c, h):
+            if h == 0:
+                grouped = work.tile([P, ROW], BF16, tag="grouped", bufs=3, align_bytes=64)
+                grouped_q[c] = grouped
+            group_pairs(turned_q[c, h], grouped_q[c][:, h * 2 * WIDTH : (h + 1) * 2 * WIDTH])
 
-        def quantise_q(g):
-            quantise(grouped_q[g][:], q_codes[:, columns(g)], q_scales[:, columns(g)])
+        def quantise_q(c):
+            quantise(grouped_q[c][:], q_codes[:, chunk_columns(c)], q_scales[:, chunk_columns(c)])
 
         products, gates, turned_ratios, grouped_y, y_operands, results = {}, {}, {}, {}, {}, {}
 
         def first_product(g):
-            acc = psum.tile([P, PACK, P], F32, tag="first_product")
+            acc = psum.tile([P, PACK, P], F32, tag="first_product", bufs=2)
             for a in range(PACK):
                 nc.tensor.matmul_mx(
                     out=acc[:, a, :],
@@ -172,41 +193,40 @@ def tile_aftfull_pb_t_kernel(tc, q, num, den, Wq, Wo, out):
 
         def sigmoid(g):
             gate = work.tile([P, P, PACK], F32, tag="gate")
-            nc.scalar.activation(
-                out=gate[:], in_=products[g][:].rearrange("p a r -> p r a"), func=FUNC.Sigmoid
-            )
+            nc.scalar.activation(out=gate[:], in_=products[g][:].rearrange("p a r -> p r a"), func=FUNC.Sigmoid)
             gates[g] = gate
 
         def turn_ratio(g):
             ratio = in_chunk(ratio_tiles, g)
-            turned = psum.tile([P, PACK, P], F32, tag="turned_ratio")
+            turned = psum.tile([P, PACK, P], F32, tag="turned", bufs=3)
             for a in range(PACK):
                 nc.tensor.transpose(turned[:, a, :], ratio[:, columns(a)], ident_f32[:])
             turned_ratios[g] = turned
 
         def apply_gate(g):
-            grouped = work.tile([P, P, PACK], BF16, tag="grouped_y", align_bytes=64)
+            if g % SUB == 0:
+                grouped = work.tile([P, SUB, P, PACK], BF16, tag="grouped_y", bufs=2, align_bytes=64)
+                grouped_y[g // SUB] = grouped
             nc.vector.tensor_tensor(
-                out=grouped[:],
+                out=grouped_y[g // SUB][:, g % SUB],
                 in0=gates[g][:],
                 in1=turned_ratios[g][:].rearrange("p a r -> p r a"),
                 op=MULT,
             )
-            grouped_y[g] = grouped
 
-        def quantise_y(g):
-            y_codes = work.tile([P, P], U32, tag="y_codes", align_bytes=64)
-            y_scales = work.tile([P, P], U8, tag="y_scales", align_bytes=64)
-            quantise(grouped_y[g][:].rearrange("p r a -> p (r a)"), y_codes[:], y_scales[:])
-            y_operands[g] = (y_codes, y_scales)
+        def quantise_y(c):
+            y_codes = work.tile([P, WIDTH], U32, tag="y_codes", bufs=2, align_bytes=64)
+            y_scales = work.tile([P, WIDTH], U8, tag="y_scales", bufs=2, align_bytes=64)
+            quantise(grouped_y[c][:].rearrange("p j r a -> p (j r a)"), y_codes[:], y_scales[:])
+            y_operands[c] = (y_codes, y_scales)
 
         def second_product(g):
-            y_codes, y_scales = y_operands[g]
-            acc = psum.tile([P, BANK], F32, tag="second_product")
+            y_codes, y_scales = y_operands[g // SUB]
+            acc = psum.tile([P, BANK], F32, tag="second_product", bufs=3)
             nc.tensor.matmul_mx(
                 out=acc[:],
-                lhsT=y_codes[:].bitcast(FP8X4),
-                lhsT_scale=y_scales[:],
+                lhsT=y_codes[:, columns(g % SUB)].bitcast(FP8X4),
+                lhsT_scale=y_scales[:, columns(g % SUB)],
                 rhs=wo_codes[:].bitcast(FP8X4),
                 rhs_scale=wo_scales[:],
                 start=True,
@@ -215,25 +235,45 @@ def tile_aftfull_pb_t_kernel(tc, q, num, den, Wq, Wo, out):
             results[g] = acc
 
         def store(g):
-            result = work.tile([P, WIDTH], F32, tag="result")
-            copy_on(g % 2 == 0, result[:], results[g][:])
+            result = work.tile([P, WIDTH], F32, tag="result", bufs=6)
+            if on_scalar(g):
+                nc.scalar.copy(out=result[:], in_=results[g][:])
+            else:
+                nc.vector.tensor_copy(out=result[:], in_=results[g][:])
             nc.sync.dma_start(out=out_groups[g // SUB, g % SUB], in_=result[:])
+
+        def on_scalar(g):
+            return g < 12 or g % 3 != 2 if g < 24 else g % 2 == 0
 
         for c in range(CHUNKS):
             root_of_den(c)
+        for c in range(2, CHUNKS):
+            fetch("num", c)
+            if c + 2 < CHUNKS:
+                fetch("q", c + 2)
         grouped_wq = group_wq()
-        grouped_wo = group_wo()
         quantise(grouped_wq[:], wq_codes[:], wq_scales[:])
+        square_chunk(0)
+        turn_q(0, 0)
+        turn_q(0, 1)
+        group_q(0, 0)
+        group_q(0, 1)
+        finish_chunk(0)
+        quantise_q(0)
+        square_chunk(1)
+        grouped_wo = group_wo()
+        turn_q(1, 0)
+        turn_q(1, 1)
+        group_q(1, 0)
+        group_q(1, 1)
         quantise(grouped_wo[:], wo_codes[:], wo_scales[:])
-        for g in range(LEAD):
-            square_root_of_den(g, on_scalar=False)
-            finish_ratio(g)
-        for g in range(LEAD):
-            turn_q(g)
-            group_q(g)
-            if g > 0:
-                quantise_q(g - 1)
-        quantise_q(LEAD - 1)
+        finish_chunk(1)
+        quantise_q(1)
+        for c in range(2, QLEAD):
+            for h in range(2):
+                turn_q(c, h)
+                group_q(c, h)
+            quantise_q(c)
 
         def is_group(g):
             return 0 <= g < GROUPS
@@ -241,14 +281,17 @@ def tile_aftfull_pb_t_kernel(tc, q, num, den, Wq, Wo, out):
         def is_new(g):
             return LEAD <= g < GROUPS
 
-        for r in range(-2, GROUPS + 2):
+        for r in range(-2, GROUPS + 6):
             new = r + LEAD
-            if is_new(new + 1):
-                turn_q(new + 1)
+            cq, step = divmod(r, SUB)
+            cq += QLEAD
+            prep = r >= 0 and cq < CHUNKS
+            if prep and step < 2:
+                turn_q(cq, step)
             if is_group(r + 1):
                 turn_ratio(r + 1)
-            if is_group(r - 1):
-                second_product(r - 1)
+            if is_group(r - 4):
+                second_product(r - 4)
             if is_group(r + 2):
                 first_product(r + 2)
             if is_group(r + 1):
@@ -257,12 +300,13 @@ def tile_aftfull_pb_t_kernel(tc, q, num, den, Wq, Wo, out):
                 apply_gate(r)
             if is_new(new):
                 square_root_of_den(new, on_scalar=True)
-                group_q(new)
             if is_new(new - 1):
                 finish_ratio(new - 1)
-            if is_group(r):
-                quantise_y(r)
-            if is_new(new - 1):
-                quantise_q(new - 1)
-            if is_group(r - 2):
-                store(r - 2)
+            if prep and 1 <= step < 3:
+                group_q(cq, step - 1)
+            if is_group(r - 5):
+                store(r - 5)
+            if is_group(r) and r % SUB == SUB - 1:
+                quantise_y(r // SUB)
+            if prep and step == 3:
+                quantise_q(cq)

@@ -20,7 +20,8 @@ SUB = 4
 CHUNKS = GROUPS // SUB
 ROW = SUB * WIDTH
 BANK = 512
-LEAD = 8
+LEAD = 13
+AHEAD = 2
 QLEAD = 4
 
 FLOPS = 2 * 2 * TOKENS * WIDTH * WIDTH
@@ -65,7 +66,10 @@ def tile_aftfull_pb_t_kernel(tc, q, num, den, Wq, Wo, out):
                 else:
                     num_rows.append(load(num_chunks[c], "den"))
             elif what == "q":
-                q_rows.append(load(q_chunks[c], "q"))
+                if c < CHUNKS // 2:
+                    q_rows.append(load(q_chunks[c], "q", bufs=CHUNKS // 2))
+                else:
+                    q_rows.append(load(q_chunks[c], "den"))
             elif what == "wq":
                 weight_rows["wq"] = load_weight(Wq, "wq")
             else:
@@ -143,23 +147,16 @@ def tile_aftfull_pb_t_kernel(tc, q, num, den, Wq, Wo, out):
             nc.scalar.activation(out=ratio[:], in_=den_rows[c][:], func=FUNC.Abs_reciprocal_sqrt)
             ratio_tiles.append(ratio)
 
-        def square_root_of_den(g, on_scalar):
+        def square_root_of_den(g):
             ratio = in_chunk(ratio_tiles, g)
-            if on_scalar:
-                nc.scalar.activation(out=ratio, in_=ratio, func=FUNC.Square)
-            else:
-                nc.vector.tensor_tensor(out=ratio, in0=ratio, in1=ratio, op=MULT)
-
-        def finish_ratio(g):
-            ratio = in_chunk(ratio_tiles, g)
-            nums = in_chunk(num_rows, g)
-            nc.vector.tensor_tensor(out=ratio, in0=nums, in1=ratio, op=MULT)
+            nc.scalar.activation(out=ratio, in_=ratio, func=FUNC.Square)
 
         def square_chunk(c):
             nc.vector.tensor_tensor(out=ratio_tiles[c][:], in0=ratio_tiles[c][:], in1=ratio_tiles[c][:], op=MULT)
 
         def finish_chunk(c):
             nc.vector.tensor_tensor(out=ratio_tiles[c][:], in0=num_rows[c][:], in1=ratio_tiles[c][:], op=MULT)
+            final_ratio[c] = ratio_tiles[c]
 
         turned_q, grouped_q = {}, {}
 
@@ -196,8 +193,19 @@ def tile_aftfull_pb_t_kernel(tc, q, num, den, Wq, Wo, out):
             nc.scalar.activation(out=gate[:], in_=products[g][:].rearrange("p a r -> p r a"), func=FUNC.Sigmoid)
             gates[g] = gate
 
+        final_ratio = {}
+
+        def stage(index, shape, dtype):
+            slot = work.tile(shape, dtype, tag="stage%d" % (index % (AHEAD + 2)), bufs=1, align_bytes=64)
+            return slot
+
+        def finish_chunk_on_gpsimd(c):
+            ratio = stage(c - AHEAD - 1, [P, ROW], F32)
+            nc.gpsimd.tensor_tensor(out=ratio[:], in0=num_rows[c][:], in1=ratio_tiles[c][:], op=MULT)
+            final_ratio[c] = ratio
+
         def turn_ratio(g):
-            ratio = in_chunk(ratio_tiles, g)
+            ratio = in_chunk(final_ratio, g)
             turned = psum.tile([P, PACK, P], F32, tag="turned", bufs=3)
             for a in range(PACK):
                 nc.tensor.transpose(turned[:, a, :], ratio[:, columns(a)], ident_f32[:])
@@ -205,7 +213,7 @@ def tile_aftfull_pb_t_kernel(tc, q, num, den, Wq, Wo, out):
 
         def apply_gate(g):
             if g % SUB == 0:
-                grouped = work.tile([P, SUB, P, PACK], BF16, tag="grouped_y", bufs=2, align_bytes=64)
+                grouped = stage(g // SUB, [P, SUB, P, PACK], BF16)
                 grouped_y[g // SUB] = grouped
             nc.vector.tensor_tensor(
                 out=grouped_y[g // SUB][:, g % SUB],
@@ -243,10 +251,11 @@ def tile_aftfull_pb_t_kernel(tc, q, num, den, Wq, Wo, out):
             nc.sync.dma_start(out=out_groups[g // SUB, g % SUB], in_=result[:])
 
         def on_scalar(g):
-            return g < 12 or g % 3 != 2 if g < 24 else g % 2 == 0
+            return g % 2 == 0
 
         for c in range(CHUNKS):
             root_of_den(c)
+        nc.scalar.activation(out=ratio_tiles[2][:], in_=ratio_tiles[2][:], func=FUNC.Square)
         for c in range(2, CHUNKS):
             fetch("num", c)
             if c + 2 < CHUNKS:
@@ -275,11 +284,13 @@ def tile_aftfull_pb_t_kernel(tc, q, num, den, Wq, Wo, out):
                 group_q(c, h)
             quantise_q(c)
 
+        finish_chunk_on_gpsimd(2)
+
         def is_group(g):
             return 0 <= g < GROUPS
 
         def is_new(g):
-            return LEAD <= g < GROUPS
+            return 12 <= g < GROUPS
 
         for r in range(-2, GROUPS + 6):
             new = r + LEAD
@@ -299,14 +310,14 @@ def tile_aftfull_pb_t_kernel(tc, q, num, den, Wq, Wo, out):
             if is_group(r):
                 apply_gate(r)
             if is_new(new):
-                square_root_of_den(new, on_scalar=True)
-            if is_new(new - 1):
-                finish_ratio(new - 1)
+                square_root_of_den(new)
             if prep and 1 <= step < 3:
                 group_q(cq, step - 1)
             if is_group(r - 5):
                 store(r - 5)
-            if is_group(r) and r % SUB == SUB - 1:
-                quantise_y(r // SUB)
             if prep and step == 3:
                 quantise_q(cq)
+            if is_group(r) and r % SUB == SUB - 1:
+                quantise_y(r // SUB)
+                if r // SUB + AHEAD + 1 < CHUNKS:
+                    finish_chunk_on_gpsimd(r // SUB + AHEAD + 1)

@@ -165,7 +165,10 @@ def tile_aftfull_pb_t_kernel(tc, q, num, den, Wq, Wo, out):
 
         def group_q(c, h):
             if h == 0:
-                grouped = work.tile([P, ROW], BF16, tag="grouped", bufs=3, align_bytes=64)
+                if c == QLEAD - 1:
+                    grouped = stage(-1, [P, ROW], BF16)
+                else:
+                    grouped = work.tile([P, ROW], BF16, tag="grouped", bufs=3, align_bytes=64)
                 grouped_q[c] = grouped
             group_pairs(turned_q[c, h], grouped_q[c][:, h * 2 * WIDTH : (h + 1) * 2 * WIDTH])
 

@@ -23,6 +23,7 @@ BANK = 512
 LEAD = 13
 AHEAD = 2
 QLEAD = 4
+IN_STAGE = {0: 2, 3: 3}
 
 FLOPS = 2 * 2 * TOKENS * WIDTH * WIDTH
 
@@ -55,6 +56,16 @@ def tile_aftfull_pb_t_kernel(tc, q, num, den, Wq, Wo, out):
             )
             return rows
 
+        def load_half(rows, source, h):
+            half = slice(h * ROW // 2, (h + 1) * ROW // 2)
+            nc.sync.dma_start(out=rows[:, half], in_=source[:, half])
+
+        def load_weight_half(rows, weight, h):
+            nc.sync.dma_start(
+                out=rows[:, h * ROW // 2 : (h + 1) * ROW // 2].rearrange("p (a k) -> p a k", a=SUB // 2),
+                in_=weight.rearrange("(a p) k -> p a k", p=P)[:, h * SUB // 2 : (h + 1) * SUB // 2, :],
+            )
+
         den_rows, num_rows, q_rows, weight_rows = [], [], [], {}
 
         def fetch(what, c):
@@ -75,10 +86,17 @@ def tile_aftfull_pb_t_kernel(tc, q, num, den, Wq, Wo, out):
             else:
                 weight_rows["wo"] = load_weight(Wo, "wo")
 
-        between = [("wq", 0), ("q", 0), ("num", 0), ("q", 1), ("wo", 0), ("num", 1), ("q", 2), ("q", 3)]
-        for c in range(CHUNKS):
-            fetch("den", c)
-            fetch(between[c][0], between[c][1])
+        first_wq = loads.tile([P, ROW], BF16, tag="wq", bufs=1)
+        first_den = loads.tile([P, ROW], BF16, tag="den", bufs=CHUNKS)
+        load_weight_half(first_wq, Wq, 0)
+        load_half(first_den, den_chunks[0], 0)
+        load_half(first_den, den_chunks[0], 1)
+        load_weight_half(first_wq, Wq, 1)
+        den_rows.append(first_den)
+        weight_rows["wq"] = first_wq
+        for what, c in [("den", 1), ("den", 2), ("q", 0), ("den", 3), ("num", 0), ("den", 4), ("den", 5),
+                        ("num", 1), ("den", 6), ("q", 1), ("q", 2), ("den", 7), ("q", 3), ("wo", 0)]:
+            fetch(what, c)
         wq_rows, wo_rows = weight_rows["wq"], weight_rows["wo"]
 
         ident_f32 = keep.tile([P, P], F32)
@@ -127,24 +145,32 @@ def tile_aftfull_pb_t_kernel(tc, q, num, den, Wq, Wo, out):
                 group_pairs(turn_pairs(wq_rows[:, half]), grouped[:, half])
             return grouped
 
-        def group_wo():
-            grouped = work.tile([P, ROW], BF16, tag="grouped", bufs=3, align_bytes=64)
-            for a in range(SUB):
-                turned = psum.tile([P, PACK, P], BF16, tag="turned", bufs=3)
-                for t in range(PACK):
-                    first = a * WIDTH + t * P
-                    nc.tensor.transpose(turned[:, t, :], wo_rows[:, first : first + P], ident_bf16[:])
-                nc.vector.tensor_copy(
-                    out=grouped[:, a * WIDTH : (a + 1) * WIDTH].rearrange("p (o t) -> p o t", t=PACK),
-                    in_=turned[:].rearrange("p t o -> p o t"),
-                )
-            return grouped
+        turned_wo, grouped_wo = {}, {}
+
+        def turn_wo(a):
+            turned = psum.tile([P, PACK, P], BF16, tag="turned", bufs=3)
+            for t in range(PACK):
+                first = a * WIDTH + t * P
+                nc.tensor.transpose(turned[:, t, :], wo_rows[:, first : first + P], ident_bf16[:])
+            turned_wo[a] = turned
+
+        def group_wo(a):
+            if a == 0:
+                grouped = work.tile([P, ROW], BF16, tag="grouped", bufs=3, align_bytes=64)
+                grouped_wo[0] = grouped
+            nc.vector.tensor_copy(
+                out=grouped_wo[0][:, a * WIDTH : (a + 1) * WIDTH].rearrange("p (o t) -> p o t", t=PACK),
+                in_=turned_wo[a][:].rearrange("p t o -> p o t"),
+            )
 
         ratio_tiles = []
 
         def root_of_den(c):
             ratio = loads.tile([P, ROW], F32, tag="ratio")
-            nc.scalar.activation(out=ratio[:], in_=den_rows[c][:], func=FUNC.Abs_reciprocal_sqrt)
+            pieces = 2 if c == 0 else 1
+            for h in range(pieces):
+                part = slice(h * ROW // pieces, (h + 1) * ROW // pieces)
+                nc.scalar.activation(out=ratio[:, part], in_=den_rows[c][:, part], func=FUNC.Abs_reciprocal_sqrt)
             ratio_tiles.append(ratio)
 
         def square_root_of_den(g):
@@ -165,8 +191,8 @@ def tile_aftfull_pb_t_kernel(tc, q, num, den, Wq, Wo, out):
 
         def group_q(c, h):
             if h == 0:
-                if c == QLEAD - 1:
-                    grouped = stage(-1, [P, ROW], BF16)
+                if c in IN_STAGE:
+                    grouped = stage(IN_STAGE[c], [P, ROW], BF16)
                 else:
                     grouped = work.tile([P, ROW], BF16, tag="grouped", bufs=3, align_bytes=64)
                 grouped_q[c] = grouped
@@ -207,6 +233,11 @@ def tile_aftfull_pb_t_kernel(tc, q, num, den, Wq, Wo, out):
             nc.gpsimd.tensor_tensor(out=ratio[:], in0=num_rows[c][:], in1=ratio_tiles[c][:], op=MULT)
             final_ratio[c] = ratio
 
+        def square_chunk_on_gpsimd(c, slot):
+            squared = stage(slot, [P, ROW], F32)
+            nc.gpsimd.tensor_tensor(out=squared[:], in0=ratio_tiles[c][:], in1=ratio_tiles[c][:], op=MULT)
+            ratio_tiles[c] = squared
+
         def turn_ratio(g):
             ratio = in_chunk(final_ratio, g)
             turned = psum.tile([P, PACK, P], F32, tag="turned", bufs=3)
@@ -225,11 +256,18 @@ def tile_aftfull_pb_t_kernel(tc, q, num, den, Wq, Wo, out):
                 op=MULT,
             )
 
-        def quantise_y(c):
-            y_codes = work.tile([P, WIDTH], U32, tag="y_codes", bufs=2, align_bytes=64)
-            y_scales = work.tile([P, WIDTH], U8, tag="y_scales", bufs=2, align_bytes=64)
-            quantise(grouped_y[c][:].rearrange("p j r a -> p (j r a)"), y_codes[:], y_scales[:])
-            y_operands[c] = (y_codes, y_scales)
+        def quantise_y(first, count):
+            c, j = divmod(first, SUB)
+            if j == 0:
+                y_codes = work.tile([P, WIDTH], U32, tag="y_codes", bufs=2, align_bytes=64)
+                y_scales = work.tile([P, WIDTH], U8, tag="y_scales", bufs=2, align_bytes=64)
+                y_operands[c] = (y_codes, y_scales)
+            y_codes, y_scales = y_operands[c]
+            quantise(
+                grouped_y[c][:, j : j + count].rearrange("p j r a -> p (j r a)"),
+                y_codes[:, j * P : (j + count) * P],
+                y_scales[:, j * P : (j + count) * P],
+            )
 
         def second_product(g):
             y_codes, y_scales = y_operands[g // SUB]
@@ -254,11 +292,10 @@ def tile_aftfull_pb_t_kernel(tc, q, num, den, Wq, Wo, out):
             nc.sync.dma_start(out=out_groups[g // SUB, g % SUB], in_=result[:])
 
         def on_scalar(g):
-            return g % 2 == 0
+            return g % 8 in (0, 2, 3, 4, 6)
 
         for c in range(CHUNKS):
             root_of_den(c)
-        nc.scalar.activation(out=ratio_tiles[2][:], in_=ratio_tiles[2][:], func=FUNC.Square)
         for c in range(2, CHUNKS):
             fetch("num", c)
             if c + 2 < CHUNKS:
@@ -271,22 +308,16 @@ def tile_aftfull_pb_t_kernel(tc, q, num, den, Wq, Wo, out):
         group_q(0, 0)
         group_q(0, 1)
         finish_chunk(0)
-        quantise_q(0)
         square_chunk(1)
-        grouped_wo = group_wo()
-        turn_q(1, 0)
-        turn_q(1, 1)
-        group_q(1, 0)
-        group_q(1, 1)
-        quantise(grouped_wo[:], wo_codes[:], wo_scales[:])
         finish_chunk(1)
-        quantise_q(1)
-        for c in range(2, QLEAD):
+        quantise_q(0)
+        square_chunk_on_gpsimd(2, IN_STAGE[0])
+        for c in range(1, QLEAD):
             for h in range(2):
                 turn_q(c, h)
                 group_q(c, h)
+        for c in range(1, QLEAD):
             quantise_q(c)
-
         finish_chunk_on_gpsimd(2)
 
         def is_group(g):
@@ -295,17 +326,25 @@ def tile_aftfull_pb_t_kernel(tc, q, num, den, Wq, Wo, out):
         def is_new(g):
             return 12 <= g < GROUPS
 
-        for r in range(-2, GROUPS + 6):
+        single = GROUPS - SUB
+
+        def product_round(g):
+            return g + 1 if g >= single else g + SUB
+
+        for r in range(-2, GROUPS + 3):
             new = r + LEAD
             cq, step = divmod(r, SUB)
             cq += QLEAD
             prep = r >= 0 and cq < CHUNKS
-            if prep and step < 2:
-                turn_q(cq, step)
             if is_group(r + 1):
                 turn_ratio(r + 1)
-            if is_group(r - 4):
-                second_product(r - 4)
+            if prep and step < 2:
+                turn_q(cq, step)
+            if -1 <= r < SUB - 1:
+                turn_wo(r + 1)
+            for g in range(GROUPS):
+                if product_round(g) == r:
+                    second_product(g)
             if is_group(r + 2):
                 first_product(r + 2)
             if is_group(r + 1):
@@ -316,11 +355,18 @@ def tile_aftfull_pb_t_kernel(tc, q, num, den, Wq, Wo, out):
                 square_root_of_den(new)
             if prep and 1 <= step < 3:
                 group_q(cq, step - 1)
-            if is_group(r - 5):
-                store(r - 5)
+            if 0 <= r < SUB:
+                group_wo(r)
+            for g in range(GROUPS):
+                if product_round(g) + 1 == r:
+                    store(g)
             if prep and step == 3:
                 quantise_q(cq)
-            if is_group(r) and r % SUB == SUB - 1:
-                quantise_y(r // SUB)
+            if r == SUB - 1:
+                quantise(grouped_wo[0][:], wo_codes[:], wo_scales[:])
+            if is_group(r) and r >= single:
+                quantise_y(r, 1)
+            elif is_group(r) and r % SUB == SUB - 1:
+                quantise_y(r - SUB + 1, SUB)
                 if r // SUB + AHEAD + 1 < CHUNKS:
                     finish_chunk_on_gpsimd(r // SUB + AHEAD + 1)

@@ -23,6 +23,8 @@ BANK = 512
 LEAD = 13
 AHEAD = 2
 QLEAD = 4
+QWAIT = 1
+VECTOR_SHARE = {6: [3], 7: [3]}
 IN_STAGE = {0: 2, 3: 3}
 
 FLOPS = 2 * 2 * TOKENS * WIDTH * WIDTH
@@ -230,8 +232,14 @@ def tile_aftfull_pb_t_kernel(tc, q, num, den, Wq, Wo, out):
 
         def finish_chunk_on_gpsimd(c):
             ratio = stage(c - AHEAD - 1, [P, ROW], F32)
-            nc.gpsimd.tensor_tensor(out=ratio[:], in0=num_rows[c][:], in1=ratio_tiles[c][:], op=MULT)
+            width = ROW - WIDTH * len(VECTOR_SHARE.get(c, []))
+            nc.gpsimd.tensor_tensor(out=ratio[:, :width], in0=num_rows[c][:, :width], in1=ratio_tiles[c][:, :width], op=MULT)
             final_ratio[c] = ratio
+
+        def finish_share_on_vector(c):
+            for j in VECTOR_SHARE.get(c, []):
+                part = slice(j * WIDTH, (j + 1) * WIDTH)
+                nc.vector.tensor_tensor(out=ratio_tiles[c][:, part], in0=num_rows[c][:, part], in1=ratio_tiles[c][:, part], op=MULT)
 
         def square_chunk_on_gpsimd(c, slot):
             squared = stage(slot, [P, ROW], F32)
@@ -239,7 +247,7 @@ def tile_aftfull_pb_t_kernel(tc, q, num, den, Wq, Wo, out):
             ratio_tiles[c] = squared
 
         def turn_ratio(g):
-            ratio = in_chunk(final_ratio, g)
+            ratio = in_chunk(ratio_tiles if g % SUB in VECTOR_SHARE.get(g // SUB, []) else final_ratio, g)
             turned = psum.tile([P, PACK, P], F32, tag="turned", bufs=3)
             for a in range(PACK):
                 nc.tensor.transpose(turned[:, a, :], ratio[:, columns(a)], ident_f32[:])
@@ -334,8 +342,8 @@ def tile_aftfull_pb_t_kernel(tc, q, num, den, Wq, Wo, out):
         for r in range(-2, GROUPS + 3):
             new = r + LEAD
             cq, step = divmod(r, SUB)
-            cq += QLEAD
-            prep = r >= 0 and cq < CHUNKS
+            cq += QLEAD - QWAIT
+            prep = QLEAD <= cq < CHUNKS
             if is_group(r + 1):
                 turn_ratio(r + 1)
             if prep and step < 2:
@@ -367,6 +375,7 @@ def tile_aftfull_pb_t_kernel(tc, q, num, den, Wq, Wo, out):
             if is_group(r) and r >= single:
                 quantise_y(r, 1)
             elif is_group(r) and r % SUB == SUB - 1:
+                finish_share_on_vector(r // SUB + AHEAD + 1)
                 quantise_y(r - SUB + 1, SUB)
                 if r // SUB + AHEAD + 1 < CHUNKS:
                     finish_chunk_on_gpsimd(r // SUB + AHEAD + 1)

@@ -350,11 +350,11 @@ def tile_aftfull_pb_t_kernel(tc, q, num, den, Wq, Wo, out):
                 turn_q(cq, step)
             if -1 <= r < SUB - 1:
                 turn_wo(r + 1)
+            if is_group(r + 2):
+                first_product(r + 2)
             for g in range(GROUPS):
                 if product_round(g) == r:
                     second_product(g)
-            if is_group(r + 2):
-                first_product(r + 2)
             if is_group(r + 1):
                 sigmoid(r + 1)
             if is_group(r):

from contextlib import ExitStack

import concourse.mybir as mybir
from concourse.masks import make_identity

BF16 = mybir.dt.bfloat16
F32 = mybir.dt.float32
U32 = mybir.dt.uint32
U8 = mybir.dt.uint8
FP8X4 = mybir.dt.float8_e4m3fn_x4
FUNC = mybir.ActivationFunctionType
MULT = mybir.AluOpType.mult

P = 128
PACK = 4
WIDTH = P * PACK
TOKENS = 4 * 1024
GROUPS = TOKENS // P
SUB = 4
CHUNKS = GROUPS // SUB
ROW = SUB * WIDTH
BANK = 512
LEAD = 13
AHEAD = 2
QLEAD = 4
QWAIT = 1
VECTOR_SHARE = {6: [3], 7: [3]}
IN_STAGE = {0: 2, 3: 3}

FLOPS = 2 * 2 * TOKENS * WIDTH * WIDTH


def tile_aftfull_pb_t_kernel(tc, q, num, den, Wq, Wo, out):
    nc = tc.nc
    by_chunk = "(c p j) w -> c p (j w)"
    q_chunks = q.flatten_outer_dims().rearrange(by_chunk, p=P, j=SUB)
    num_chunks = num.flatten_outer_dims().rearrange(by_chunk, p=P, j=SUB)
    den_chunks = den.flatten_outer_dims().rearrange(by_chunk, p=P, j=SUB)
    out_groups = out.flatten_outer_dims().rearrange("(c p j) w -> c j p w", p=P, j=SUB)

    with ExitStack() as ctx:
        keep = ctx.enter_context(tc.tile_pool(name="keep", bufs=1))
        loads = ctx.enter_context(tc.tile_pool(name="loads", bufs=CHUNKS))
        work = ctx.enter_context(tc.tile_pool(name="work", bufs=4))
        psum = ctx.enter_context(tc.psum_pool(name="psum", bufs=2))
        ctx.enter_context(tc.manual_schedule())

        def load(source, tag, bufs=CHUNKS):
            rows = loads.tile([P, ROW], BF16, tag=tag, bufs=bufs)
            nc.sync.dma_start(out=rows[:], in_=source)
            return rows

        def load_weight(weight, tag):
            rows = loads.tile([P, ROW], BF16, tag=tag, bufs=1)
            nc.sync.dma_start(
                out=rows[:].rearrange("p (a k) -> p a k", a=SUB),
                in_=weight.rearrange("(a p) k -> p a k", p=P),
            )
            return rows

        def load_half(rows, source, h):
            half = slice(h * ROW // 2, (h + 1) * ROW // 2)
            nc.sync.dma_start(out=rows[:, half], in_=source[:, half])

        def load_weight_half(rows, weight, h):
            nc.sync.dma_start(
                out=rows[:, h * ROW // 2 : (h + 1) * ROW // 2].rearrange("p (a k) -> p a k", a=SUB // 2),
                in_=weight.rearrange("(a p) k -> p a k", p=P)[:, h * SUB // 2 : (h + 1) * SUB // 2, :],
            )

        den_rows, num_rows, q_rows, weight_rows = [], [], [], {}

        def fetch(what, c):
            if what == "den":
                den_rows.append(load(den_chunks[c], "den"))
            elif what == "num":
                if c < CHUNKS // 2:
                    num_rows.append(load(num_chunks[c], "num", bufs=CHUNKS // 2))
                else:
                    num_rows.append(load(num_chunks[c], "den"))
            elif what == "q":
                if c < CHUNKS // 2:
                    q_rows.append(load(q_chunks[c], "q", bufs=CHUNKS // 2))
                else:
                    q_rows.append(load(q_chunks[c], "den"))
            elif what == "wq":
                weight_rows["wq"] = load_weight(Wq, "wq")
            else:
                weight_rows["wo"] = load_weight(Wo, "wo")

        first_wq = loads.tile([P, ROW], BF16, tag="wq", bufs=1)
        first_den = loads.tile([P, ROW], BF16, tag="den", bufs=CHUNKS)
        load_weight_half(first_wq, Wq, 0)
        load_half(first_den, den_chunks[0], 0)
        load_half(first_den, den_chunks[0], 1)
        load_weight_half(first_wq, Wq, 1)
        den_rows.append(first_den)
        weight_rows["wq"] = first_wq
        for what, c in [("den", 1), ("den", 2), ("q", 0), ("den", 3), ("num", 0), ("den", 4), ("den", 5),
                        ("num", 1), ("den", 6), ("q", 1), ("q", 2), ("den", 7), ("q", 3), ("wo", 0)]:
            fetch(what, c)
        wq_rows, wo_rows = weight_rows["wq"], weight_rows["wo"]

        ident_f32 = keep.tile([P, P], F32)
        make_identity(nc, ident_f32[:])
        ident_bf16 = keep.tile([P, P], BF16)
        make_identity(nc, ident_bf16[:])

        wq_codes = keep.tile([P, WIDTH], U32, align_bytes=64)
        wq_scales = keep.tile([P, WIDTH], U8, align_bytes=64)
        wo_codes = keep.tile([P, WIDTH], U32, align_bytes=64)
        wo_scales = keep.tile([P, WIDTH], U8, align_bytes=64)
        q_codes = keep.tile([P, TOKENS], U32, align_bytes=64)
        q_scales = keep.tile([P, TOKENS], U8, align_bytes=64)

        def quantise(grouped, codes, scales):
            nc.vector.quantize_mx(out=codes.bitcast(FP8X4), scales=scales, in_=grouped)

        def columns(g):
            return slice(g * P, (g + 1) * P)

        def chunk_columns(c):
            return slice(c * WIDTH, (c + 1) * WIDTH)

        def in_chunk(tiles, g):
            return tiles[g // SUB][:, (g % SUB) * WIDTH : (g % SUB + 1) * WIDTH]

        def turn_pairs(rows):
            words = rows.bitcast(F32)
            turned = psum.tile([P, 2, 2, P], F32, tag="turned", bufs=3)
            for b in range(2):
                for u in range(2):
                    first = b * 2 * P + u * P
                    nc.tensor.transpose(turned[:, b, u, :], words[:, first : first + P], ident_f32[:])
            return turned

        def group_pairs(turned, grouped):
            nc.vector.tensor_copy(
                out=grouped.bitcast(F32).rearrange("p (b r u) -> p b r u", b=2, u=2),
                in_=turned[:].rearrange("p b u r -> p b r u"),
            )

        def group_wq():
            grouped = work.tile([P, ROW], BF16, tag="grouped", bufs=3, align_bytes=64)
            for h in range(2):
                half = slice(h * 2 * WIDTH, (h + 1) * 2 * WIDTH)
                group_pairs(turn_pairs(wq_rows[:, half]), grouped[:, half])
            return grouped

        turned_wo, grouped_wo = {}, {}

        def turn_wo(a):
            turned = psum.tile([P, PACK, P], BF16, tag="turned", bufs=3)
            for t in range(PACK):
                first = a * WIDTH + t * P
                nc.tensor.transpose(turned[:, t, :], wo_rows[:, first : first + P], ident_bf16[:])
            turned_wo[a] = turned

        def group_wo(a):
            if a == 0:
                grouped = work.tile([P, ROW], BF16, tag="grouped", bufs=3, align_bytes=64)
                grouped_wo[0] = grouped
            nc.vector.tensor_copy(
                out=grouped_wo[0][:, a * WIDTH : (a + 1) * WIDTH].rearrange("p (o t) -> p o t", t=PACK),
                in_=turned_wo[a][:].rearrange("p t o -> p o t"),
            )

        ratio_tiles = []

        def root_of_den(c):
            ratio = loads.tile([P, ROW], F32, tag="ratio")
            pieces = 2 if c == 0 else 1
            for h in range(pieces):
                part = slice(h * ROW // pieces, (h + 1) * ROW // pieces)
                nc.scalar.activation(out=ratio[:, part], in_=den_rows[c][:, part], func=FUNC.Abs_reciprocal_sqrt)
            ratio_tiles.append(ratio)

        def square_root_of_den(g):
            ratio = in_chunk(ratio_tiles, g)
            nc.scalar.activation(out=ratio, in_=ratio, func=FUNC.Square)

        def square_chunk(c):
            nc.vector.tensor_tensor(out=ratio_tiles[c][:], in0=ratio_tiles[c][:], in1=ratio_tiles[c][:], op=MULT)

        def finish_chunk(c):
            nc.vector.tensor_tensor(out=ratio_tiles[c][:], in0=num_rows[c][:], in1=ratio_tiles[c][:], op=MULT)
            final_ratio[c] = ratio_tiles[c]

        turned_q, grouped_q = {}, {}

        def turn_q(c, h):
            turned_q[c, h] = turn_pairs(q_rows[c][:, h * 2 * WIDTH : (h + 1) * 2 * WIDTH])

        def group_q(c, h):
            if h == 0:
                if c in IN_STAGE:
                    grouped = stage(IN_STAGE[c], [P, ROW], BF16)
                else:
                    grouped = work.tile([P, ROW], BF16, tag="grouped", bufs=3, align_bytes=64)
                grouped_q[c] = grouped
            group_pairs(turned_q[c, h], grouped_q[c][:, h * 2 * WIDTH : (h + 1) * 2 * WIDTH])

        def quantise_q(c):
            quantise(grouped_q[c][:], q_codes[:, chunk_columns(c)], q_scales[:, chunk_columns(c)])

        products, gates, turned_ratios, grouped_y, y_operands, results = {}, {}, {}, {}, {}, {}

        def first_product(g):
            acc = psum.tile([P, PACK, P], F32, tag="first_product", bufs=2)
            for a in range(PACK):
                nc.tensor.matmul_mx(
                    out=acc[:, a, :],
                    lhsT=wq_codes[:, columns(a)].bitcast(FP8X4),
                    lhsT_scale=wq_scales[:, columns(a)],
                    rhs=q_codes[:, columns(g)].bitcast(FP8X4),
                    rhs_scale=q_scales[:, columns(g)],
                    start=True,
                    stop=True,
                )
            products[g] = acc

        def sigmoid(g):
            gate = work.tile([P, P, PACK], F32, tag="gate")
            nc.scalar.activation(out=gate[:], in_=products[g][:].rearrange("p a r -> p r a"), func=FUNC.Sigmoid)
            gates[g] = gate

        final_ratio = {}

        def stage(index, shape, dtype):
            slot = work.tile(shape, dtype, tag="stage%d" % (index % (AHEAD + 2)), bufs=1, align_bytes=64)
            return slot

        def finish_chunk_on_gpsimd(c):
            ratio = stage(c - AHEAD - 1, [P, ROW], F32)
            width = ROW - WIDTH * len(VECTOR_SHARE.get(c, []))
            nc.gpsimd.tensor_tensor(out=ratio[:, :width], in0=num_rows[c][:, :width], in1=ratio_tiles[c][:, :width], op=MULT)
            final_ratio[c] = ratio

        def finish_share_on_vector(c):
            for j in VECTOR_SHARE.get(c, []):
                part = slice(j * WIDTH, (j + 1) * WIDTH)
                nc.vector.tensor_tensor(out=ratio_tiles[c][:, part], in0=num_rows[c][:, part], in1=ratio_tiles[c][:, part], op=MULT)

        def square_chunk_on_gpsimd(c, slot):
            squared = stage(slot, [P, ROW], F32)
            nc.gpsimd.tensor_tensor(out=squared[:], in0=ratio_tiles[c][:], in1=ratio_tiles[c][:], op=MULT)
            ratio_tiles[c] = squared

        def turn_ratio(g):
            ratio = in_chunk(ratio_tiles if g % SUB in VECTOR_SHARE.get(g // SUB, []) else final_ratio, g)
            turned = psum.tile([P, PACK, P], F32, tag="turned", bufs=3)
            for a in range(PACK):
                nc.tensor.transpose(turned[:, a, :], ratio[:, columns(a)], ident_f32[:])
            turned_ratios[g] = turned

        def apply_gate(g):
            if g % SUB == 0:
                grouped = stage(g // SUB, [P, SUB, P, PACK], BF16)
                grouped_y[g // SUB] = grouped
            nc.vector.tensor_tensor(
                out=grouped_y[g // SUB][:, g % SUB],
                in0=gates[g][:],
                in1=turned_ratios[g][:].rearrange("p a r -> p r a"),
                op=MULT,
            )

        def quantise_y(first, count):
            c, j = divmod(first, SUB)
            if j == 0:
                y_codes = work.tile([P, WIDTH], U32, tag="y_codes", bufs=2, align_bytes=64)
                y_scales = work.tile([P, WIDTH], U8, tag="y_scales", bufs=2, align_bytes=64)
                y_operands[c] = (y_codes, y_scales)
            y_codes, y_scales = y_operands[c]
            quantise(
                grouped_y[c][:, j : j + count].rearrange("p j r a -> p (j r a)"),
                y_codes[:, j * P : (j + count) * P],
                y_scales[:, j * P : (j + count) * P],
            )

        def second_product(g):
            y_codes, y_scales = y_operands[g // SUB]
            acc = psum.tile([P, BANK], F32, tag="second_product", bufs=3)
            nc.tensor.matmul_mx(
                out=acc[:],
                lhsT=y_codes[:, columns(g % SUB)].bitcast(FP8X4),
                lhsT_scale=y_scales[:, columns(g % SUB)],
                rhs=wo_codes[:].bitcast(FP8X4),
                rhs_scale=wo_scales[:],
                start=True,
                stop=True,
            )
            results[g] = acc

        def store(g):
            result = work.tile([P, WIDTH], F32, tag="result", bufs=6)
            if on_scalar(g):
                nc.scalar.copy(out=result[:], in_=results[g][:])
            else:
                nc.vector.tensor_copy(out=result[:], in_=results[g][:])
            nc.sync.dma_start(out=out_groups[g // SUB, g % SUB], in_=result[:])

        def on_scalar(g):
            return g % 8 in (0, 2, 3, 4, 6)

        for c in range(CHUNKS):
            root_of_den(c)
        for c in range(2, CHUNKS):
            fetch("num", c)
            if c + 2 < CHUNKS:
                fetch("q", c + 2)
        grouped_wq = group_wq()
        quantise(grouped_wq[:], wq_codes[:], wq_scales[:])
        square_chunk(0)
        turn_q(0, 0)
        turn_q(0, 1)
        group_q(0, 0)
        group_q(0, 1)
        finish_chunk(0)
        square_chunk(1)
        finish_chunk(1)
        quantise_q(0)
        square_chunk_on_gpsimd(2, IN_STAGE[0])
        for c in range(1, QLEAD):
            for h in range(2):
                turn_q(c, h)
                group_q(c, h)
        for c in range(1, QLEAD):
            quantise_q(c)
        finish_chunk_on_gpsimd(2)

        def is_group(g):
            return 0 <= g < GROUPS

        def is_new(g):
            return 12 <= g < GROUPS

        single = GROUPS - SUB

        def product_round(g):
            return g + 1 if g >= single else g + SUB

        for r in range(-2, GROUPS + 3):
            new = r + LEAD
            cq, step = divmod(r, SUB)
            cq += QLEAD - QWAIT
            prep = QLEAD <= cq < CHUNKS
            if is_group(r + 1):
                turn_ratio(r + 1)
            if prep and step < 2:
                turn_q(cq, step)
            if -1 <= r < SUB - 1:
                turn_wo(r + 1)
            if is_group(r + 2):
                first_product(r + 2)
            for g in range(GROUPS):
                if product_round(g) == r:
                    second_product(g)
            if is_group(r + 1):
                sigmoid(r + 1)
            if is_group(r):
                apply_gate(r)
            if is_new(new):
                square_root_of_den(new)
            if prep and 1 <= step < 3:
                group_q(cq, step - 1)
            if 0 <= r < SUB:
                group_wo(r)
            for g in range(GROUPS):
                if product_round(g) + 1 == r:
                    store(g)
            if prep and step == 3:
                quantise_q(cq)
            if r == SUB - 1:
                quantise(grouped_wo[0][:], wo_codes[:], wo_scales[:])
            if is_group(r) and r >= single:
                quantise_y(r, 1)
            elif is_group(r) and r % SUB == SUB - 1:
                finish_share_on_vector(r // SUB + AHEAD + 1)
                quantise_y(r - SUB + 1, SUB)
                if r // SUB + AHEAD + 1 < CHUNKS:
                    finish_chunk_on_gpsimd(r // SUB + AHEAD + 1)
